import numpy as np
import ml_dtypes


def mxq(x, axis, fmt="e4m3"):
    dtype, down = {"e4m3": (ml_dtypes.float8_e4m3fn, 7), "e5m2": (ml_dtypes.float8_e5m2, 14)}[fmt]
    v = np.moveaxis(np.asarray(x, np.float32).astype(ml_dtypes.bfloat16).astype(np.float64), axis, -1)
    blocks = v.reshape(v.shape[:-1] + (-1, 32))
    amax = np.abs(blocks).max(-1, keepdims=True)
    byte = np.maximum(np.where(amax > 0, np.frexp(amax)[1] - 1 + 127, 0) - down, 1)
    scale = np.exp2(byte - 127.0)
    codes = (blocks / scale).astype(np.float32).astype(dtype).astype(np.float64)
    return np.moveaxis((codes * scale).reshape(v.shape), -1, axis)


WIDE = False


def mx_kscale(k):
    if not WIDE:
        return np.ones(k)
    levels = np.array([10, -10, 5, -5, 0])
    a = np.random.permutation(np.resize(levels, k // 512 * 4)).reshape(k // 512, 4)
    idx = np.arange(k)
    return np.exp2(a[idx // 512, idx % 128 // 32])


BF16 = ml_dtypes.bfloat16


def bf(x):
    return np.asarray(x, np.float32).astype(BF16)


def f64(x):
    return np.asarray(x).astype(np.float64)


B, S, DIM, N_HEADS, Q_LORA, KV_LORA, NOPE, ROPE, V_HEAD = 4, 1024, 1024, 2, 512, 512, 128, 64, 128
QK_HEAD = NOPE + ROPE
EPS = 1e-6


def rmsnorm(v, w):
    return v * (1.0 / np.sqrt(np.mean(v * v, axis=-1, keepdims=True) + EPS)) * w


def apply_rope(v, cos, sin):
    vr = v.reshape(v.shape[:-1] + (-1, 2))
    c = cos[None, :, None, :]
    s = sin[None, :, None, :]
    re = vr[..., 0] * c - vr[..., 1] * s
    im = vr[..., 0] * s + vr[..., 1] * c
    return np.stack([re, im], axis=-1).reshape(v.shape)


def setup_inputs():
    s, t = mx_kscale(DIM), mx_kscale(Q_LORA)
    inv_freq = 1.0 / (10000.0 ** (np.arange(0, ROPE, 2) / ROPE))
    ang = np.arange(S)[:, None] * inv_freq[None, :]
    return {"x": bf(np.random.standard_normal((B, S, DIM)) * s),
            "freqs_cos": bf(np.cos(ang)),
            "freqs_sin": bf(np.sin(ang)),
            "wq_a": bf(np.random.standard_normal((Q_LORA, DIM)) / np.sqrt(DIM) / s),
            "q_norm_w": bf((1.0 + 0.1 * np.random.standard_normal(Q_LORA)) * t),
            "wq_b": bf(np.random.standard_normal((N_HEADS * QK_HEAD, Q_LORA)) / np.sqrt(Q_LORA) / t)}


def reference(x, freqs_cos, freqs_sin, wq_a, q_norm_w, wq_b):
    ql = mxq(f64(x), 2, "e4m3") @ mxq(f64(wq_a), 1, "e4m3").T
    qn = rmsnorm(ql, f64(q_norm_w))
    q = mxq(qn, 2, "e4m3") @ mxq(f64(wq_b), 1, "e4m3").T
    q = q.reshape(B, S, N_HEADS, QK_HEAD)
    q_nope = np.ascontiguousarray(q[..., :NOPE])
    q_pe = apply_rope(q[..., NOPE:], f64(freqs_cos), f64(freqs_sin))
    return q_nope, q_pe

@@ -1,0 +1,314 @@
+from contextlib import ExitStack
+
+import concourse.mybir as mybir
+from concourse.masks import make_identity
+
+F32 = mybir.dt.float32
+BF16 = mybir.dt.bfloat16
+U32 = mybir.dt.uint32
+U8 = mybir.dt.uint8
+FP8X4 = mybir.dt.float8_e4m3fn_x4
+ACT = mybir.ActivationFunctionType
+ALU = mybir.AluOpType
+
+P = 128
+PACK = 4
+K_PASS = P * PACK
+
+BATCH, SEQ, DIM = 4, 1024, 1024
+Q_LORA = 512
+HEADS, NOPE, ROPE = 2, 128, 64
+EPS = 1e-6
+
+SEQ_TILES = SEQ // P
+PASSES_1 = DIM // K_PASS
+WORD_BLOCKS = DIM // 2 // P
+NOPE_COLS = HEADS * NOPE
+ROPE_COLS = HEADS * ROPE
+Q_COLS = NOPE_COLS + 2 * ROPE_COLS
+
+ROUND_TILES = 2
+ROUNDS = BATCH * SEQ_TILES // ROUND_TILES
+ROUNDS_PER_BATCH = SEQ_TILES // ROUND_TILES
+
+PRODUCT_1_LAG = 1
+NORMALISE_LAG = 2
+TURN_QN_LAG = 3
+PRODUCT_2_LAG = 4
+FINISH_LAG = 5
+
+FLOPS = 2 * BATCH * SEQ * (DIM * Q_LORA + Q_LORA * HEADS * (NOPE + ROPE))
+
+
+def tile_mla_pa_t_kernel(
+    tc, x, freqs_cos, freqs_sin, wq_a, q_norm_w, wq_b, out_0, out_1
+):
+    nc = tc.nc
+
+    x_view = x.rearrange("b (p s) k -> b p s k", s=SEQ_TILES)
+    nope_view = out_0.rearrange("b (p s) h d -> b p s (h d)", s=SEQ_TILES)
+    rope_view = out_1.rearrange("b (p s) h d -> b p s (h d)", s=SEQ_TILES)
+
+    with ExitStack() as ctx:
+        ctx.enter_context(tc.manual_schedule())
+
+        keep = ctx.enter_context(tc.tile_pool(name="keep", bufs=1))
+        stage = ctx.enter_context(tc.tile_pool(name="stage", bufs=2))
+        ring = ctx.enter_context(tc.tile_pool(name="ring", bufs=3))
+        ps_words = ctx.enter_context(tc.psum_pool(name="ps_words", bufs=2))
+        ps_ql = ctx.enter_context(tc.psum_pool(name="ps_ql", bufs=3))
+        ps_qnt = ctx.enter_context(tc.psum_pool(name="ps_qnt", bufs=1))
+        ps_q = ctx.enter_context(tc.psum_pool(name="ps_q", bufs=2))
+
+        wa_rows = keep.tile([P, PACK, DIM], BF16)
+        nc.sync.dma_start(out=wa_rows[:], in_=wq_a.rearrange("(r t) k -> r t k", t=PACK))
+
+        x_rows = []
+        for r in range(ROUNDS):
+            x_round = keep.tile([P, ROUND_TILES, DIM], BF16, name="x_round%d" % r)
+            x_rows.append(x_round)
+
+        def load_x(r):
+            b, s0 = r // ROUNDS_PER_BATCH, (r % ROUNDS_PER_BATCH) * ROUND_TILES
+            nc.sync.dma_start(out=x_rows[r][:], in_=x_view[b, :, s0 : s0 + ROUND_TILES, :])
+
+        load_x(0)
+        load_x(1)
+
+        wb_rows = keep.tile([P, 3, Q_LORA], BF16)
+        wb_heads = wq_b.rearrange("(h d) k -> d h k", h=HEADS)
+        nc.sync.dma_start(out=wb_rows[:, 0:HEADS, :], in_=wb_heads[0:NOPE, :, :])
+        for h in range(HEADS):
+            nc.sync.dma_start(
+                out=wb_rows[h * ROPE : (h + 1) * ROPE, HEADS, :],
+                in_=wb_heads[NOPE : NOPE + ROPE, h, :],
+            )
+        for r in range(2, ROUNDS):
+            load_x(r)
+
+        cos_rows = keep.tile([P, SEQ_TILES, ROPE // 2], BF16)
+        sin_rows = keep.tile([P, SEQ_TILES, ROPE // 2], BF16)
+        gain_rows = keep.tile([P, Q_LORA], BF16)
+        nc.scalar.dma_start(out=gain_rows[:], in_=q_norm_w.partition_broadcast(P))
+        nc.scalar.dma_start(
+            out=cos_rows[:], in_=freqs_cos.rearrange("(p s) j -> p s j", s=SEQ_TILES)
+        )
+        nc.scalar.dma_start(
+            out=sin_rows[:], in_=freqs_sin.rearrange("(p s) j -> p s j", s=SEQ_TILES)
+        )
+
+        ident_f32 = keep.tile([P, P], F32)
+        make_identity(nc, ident_f32[:])
+        ident_bf16 = keep.tile([P, P], BF16)
+        make_identity(nc, ident_bf16[:])
+
+        warm = keep.tile([P, 1], F32)
+        nc.scalar.activation(out=warm[:], in_=ident_f32[:, 0:1], func=ACT.Sqrt)
+
+        gain = keep.tile([P, Q_LORA], F32)
+        nc.gpsimd.tensor_copy(
+            out=gain[:].rearrange("p (t r) -> p t r", t=PACK),
+            in_=gain_rows[:].rearrange("p (r t) -> p t r", t=PACK),
+        )
+
+        rot = keep.tile([P, SEQ_TILES, 2, ROPE], F32)
+        rot_pairs = rot[:].rearrange("p s c (j e) -> p s c j e", e=2)
+        nc.gpsimd.tensor_copy(out=rot_pairs[:, :, 0, :, 0], in_=cos_rows[:])
+        nc.gpsimd.tensor_copy(out=rot_pairs[:, :, 0, :, 1], in_=cos_rows[:])
+        nc.gpsimd.tensor_scalar_mul(out=rot_pairs[:, :, 1, :, 0], in0=sin_rows[:], scalar1=-1.0)
+        nc.gpsimd.tensor_copy(out=rot_pairs[:, :, 1, :, 1], in_=sin_rows[:])
+
+        def turn_words(bank, word_blocks):
+            for i, block in enumerate(word_blocks):
+                nc.tensor.transpose(bank[:, i, :], block, ident_f32[:])
+
+        wa_grouped = keep.tile([P, PASSES_1 * Q_LORA * PACK], BF16, align_bytes=64)
+        wa_grouped_words = wa_grouped[:].bitcast(F32).rearrange(
+            "p (g n u) -> p g n u", g=PASSES_1, u=2
+        )
+        for t in range(PACK):
+            words = wa_rows[:, t, :].bitcast(F32)
+            bank = ps_words.tile([P, WORD_BLOCKS, P], F32, tag="words")
+            turn_words(bank, [words[:, i * P : (i + 1) * P] for i in range(WORD_BLOCKS)])
+            nc.vector.tensor_copy(
+                out=wa_grouped_words[:, :, t * P : (t + 1) * P, :],
+                in_=bank[:].rearrange("p (g u) r -> p g r u", u=2),
+            )
+        wa_codes = keep.tile([P, PASSES_1 * Q_LORA], U32, align_bytes=64)
+        wa_scales = keep.tile([P, PASSES_1 * Q_LORA], U8, align_bytes=64)
+        nc.vector.quantize_mx(
+            out=wa_codes[:].bitcast(FP8X4), scales=wa_scales[:], in_=wa_grouped[:]
+        )
+
+        wb_grouped = keep.tile([P, Q_COLS * PACK], BF16, align_bytes=64)
+        wb_grouped_words = wb_grouped[:].bitcast(F32).rearrange("p (n u) -> p n u", u=2)
+
+        def wb_word_blocks(c):
+            words = wb_rows[:, c, :].bitcast(F32).rearrange("r (p u) -> r u p", u=2)
+            return [words[:, u, :] for u in range(2)]
+
+        bank = ps_words.tile([P, 2 * HEADS, P], F32, tag="words")
+        turn_words(bank, wb_word_blocks(0) + wb_word_blocks(1))
+        nc.vector.tensor_copy(
+            out=wb_grouped_words[:, 0:NOPE_COLS, :].rearrange("p (c r) u -> p c r u", c=HEADS),
+            in_=bank[:].rearrange("p (c u) r -> p c r u", u=2),
+        )
+        bank = ps_words.tile([P, 2, P], F32, tag="words")
+        turn_words(bank, wb_word_blocks(HEADS))
+        nc.vector.tensor_copy(
+            out=wb_grouped_words[:, NOPE_COLS : NOPE_COLS + ROPE_COLS, :],
+            in_=bank[:].rearrange("p u r -> p r u"),
+        )
+        swapped = wb_grouped_words[:, NOPE_COLS + ROPE_COLS : Q_COLS, :].rearrange(
+            "p (m e) u -> p m e u", e=2
+        )
+        pairs = bank[:].rearrange("p u (m e) -> p m e u", e=2)
+        for e in range(2):
+            nc.vector.tensor_copy(out=swapped[:, :, 1 - e, :], in_=pairs[:, :, e, :])
+        wb_codes = keep.tile([P, Q_COLS], U32, align_bytes=64)
+        wb_scales = keep.tile([P, Q_COLS], U8, align_bytes=64)
+        nc.vector.quantize_mx(
+            out=wb_codes[:].bitcast(FP8X4), scales=wb_scales[:], in_=wb_grouped[:]
+        )
+
+        x_grouped, x_mx, ql_banks, rms_of = {}, {}, {}, {}
+        qn_of, qn_grouped, qn_mx, q_banks = {}, {}, {}, {}
+
+        def turn_x(r):
+            grouped = stage.tile([P, ROUND_TILES * DIM], BF16, align_bytes=64, tag="x_grouped")
+            grouped_words = grouped[:].bitcast(F32).rearrange(
+                "p (j g r u) -> p j g r u", j=ROUND_TILES, g=PASSES_1, u=2
+            )
+            for j in range(ROUND_TILES):
+                words = x_rows[r][:, j, :].bitcast(F32)
+                bank = ps_words.tile([P, WORD_BLOCKS, P], F32, tag="words")
+                turn_words(bank, [words[:, i * P : (i + 1) * P] for i in range(WORD_BLOCKS)])
+                nc.scalar.copy(
+                    out=grouped_words[:, j], in_=bank[:].rearrange("p (g u) r -> p g r u", u=2)
+                )
+            x_grouped[r] = grouped
+
+        def quantise_x(r):
+            codes = ring.tile([P, ROUND_TILES * PASSES_1 * P], U32, align_bytes=64, tag="x_codes")
+            scales = ring.tile([P, ROUND_TILES * PASSES_1 * P], U8, align_bytes=64, tag="x_scales")
+            nc.vector.quantize_mx(
+                out=codes[:].bitcast(FP8X4), scales=scales[:], in_=x_grouped[r][:]
+            )
+            x_mx[r] = (codes, scales)
+
+        def product_1(r):
+            codes, scales = x_mx[r]
+            sum_sq = ring.tile([P, ROUND_TILES], F32, tag="sum_sq")
+            ql_banks[r] = []
+            for j in range(ROUND_TILES):
+                ql = ps_ql.tile([P, Q_LORA], F32, tag="ql")
+                for g in range(PASSES_1):
+                    tok = slice((j * PASSES_1 + g) * P, (j * PASSES_1 + g + 1) * P)
+                    col = slice(g * Q_LORA, (g + 1) * Q_LORA)
+                    nc.tensor.matmul_mx(
+                        out=ql[:],
+                        lhsT=codes[:, tok].bitcast(FP8X4),
+                        lhsT_scale=scales[:, tok],
+                        rhs=wa_codes[:, col].bitcast(FP8X4),
+                        rhs_scale=wa_scales[:, col],
+                        start=(g == 0),
+                        stop=(g == PASSES_1 - 1),
+                    )
+                squares = stage.tile([P, Q_LORA], BF16, tag="squares")
+                nc.scalar.activation(
+                    out=squares[:], in_=ql[:], func=ACT.Square, accum_out=sum_sq[:, j : j + 1]
+                )
+                ql_banks[r].append(ql)
+            rms = ring.tile([P, ROUND_TILES], F32, tag="rms")
+            nc.scalar.activation(
+                out=rms[:], in_=sum_sq[:], func=ACT.Sqrt, bias=EPS, scale=1.0 / Q_LORA
+            )
+            rms_of[r] = rms
+
+        def normalise(r):
+            rstd = ring.tile([P, ROUND_TILES], F32, tag="rstd")
+            nc.vector.reciprocal(out=rstd[:], in_=rms_of[r][:])
+            qn = ring.tile([P, ROUND_TILES, Q_LORA], BF16, tag="qn")
+            for j in range(ROUND_TILES):
+                nc.vector.scalar_tensor_tensor(
+                    out=qn[:, j, :],
+                    in0=ql_banks[r][j][:],
+                    scalar=rstd[:, j : j + 1],
+                    in1=gain[:],
+                    op0=ALU.mult,
+                    op1=ALU.mult,
+                )
+            qn_of[r] = qn
+
+        def turn_qn(r):
+            qnt = ps_qnt.tile([P, ROUND_TILES, PACK, P], BF16, tag="qnt")
+            for j in range(ROUND_TILES):
+                for t in range(PACK):
+                    nc.tensor.transpose(
+                        qnt[:, j, t, :], qn_of[r][:, j, t * P : (t + 1) * P], ident_bf16[:]
+                    )
+            grouped = stage.tile([P, ROUND_TILES * Q_LORA], BF16, align_bytes=64, tag="qn_grouped")
+            nc.scalar.copy(
+                out=grouped[:].rearrange("p (j r t) -> p j r t", j=ROUND_TILES, t=PACK),
+                in_=qnt[:].rearrange("p j t r -> p j r t"),
+            )
+            qn_grouped[r] = grouped
+
+        def quantise_qn(r):
+            codes = ring.tile([P, ROUND_TILES * P], U32, align_bytes=64, tag="qn_codes")
+            scales = ring.tile([P, ROUND_TILES * P], U8, align_bytes=64, tag="qn_scales")
+            nc.vector.quantize_mx(
+                out=codes[:].bitcast(FP8X4), scales=scales[:], in_=qn_grouped[r][:]
+            )
+            qn_mx[r] = (codes, scales)
+
+        def product_2(r):
+            codes, scales = qn_mx[r]
+            q_banks[r] = []
+            for j in range(ROUND_TILES):
+                tok = slice(j * P, (j + 1) * P)
+                q = ps_q.tile([P, Q_COLS], F32, tag="q")
+                nc.tensor.matmul_mx(
+                    out=q[:],
+                    lhsT=codes[:, tok].bitcast(FP8X4),
+                    lhsT_scale=scales[:, tok],
+                    rhs=wb_codes[:].bitcast(FP8X4),
+                    rhs_scale=wb_scales[:],
+                    start=True,
+                    stop=True,
+                )
+                q_banks[r].append(q)
+
+        def finish(r):
+            b, s0 = r // ROUNDS_PER_BATCH, (r % ROUNDS_PER_BATCH) * ROUND_TILES
+            nope = ring.tile([P, ROUND_TILES, NOPE_COLS], F32, tag="nope")
+            terms = ring.tile([P, ROUND_TILES, 2, ROPE_COLS], F32, tag="terms")
+            rope = ring.tile([P, ROUND_TILES, ROPE_COLS], F32, tag="rope")
+            for j in range(ROUND_TILES):
+                q = q_banks[r][j]
+                nc.vector.tensor_copy(out=nope[:, j, :], in_=q[:, 0:NOPE_COLS])
+                nc.vector.tensor_tensor(
+                    out=terms[:, j].rearrange("p c (h d) -> p c h d", h=HEADS),
+                    in0=q[:, NOPE_COLS:Q_COLS].rearrange("p (c h d) -> p c h d", c=2, h=HEADS),
+                    in1=rot[:, s0 + j].unsqueeze(2).to_broadcast([P, 2, HEADS, ROPE]),
+                    op=ALU.mult,
+                )
+            nc.gpsimd.tensor_tensor(
+                out=rope[:], in0=terms[:, :, 0, :], in1=terms[:, :, 1, :], op=ALU.add
+            )
+            nc.sync.dma_start(out=nope_view[b, :, s0 : s0 + ROUND_TILES, :], in_=nope[:])
+            nc.sync.dma_start(out=rope_view[b, :, s0 : s0 + ROUND_TILES, :], in_=rope[:])
+
+        def run(stage_fn, r):
+            if 0 <= r < ROUNDS:
+                stage_fn(r)
+
+        for i in range(ROUNDS + FINISH_LAG):
+            run(finish, i - FINISH_LAG)
+            run(normalise, i - NORMALISE_LAG)
+            run(turn_x, i)
+            run(turn_qn, i - TURN_QN_LAG)
+            run(quantise_x, i)
+            run(quantise_qn, i - TURN_QN_LAG)
+            run(product_1, i - PRODUCT_1_LAG)
+            run(product_2, i - PRODUCT_2_LAG)

@@ -36,6 +36,8 @@ NORMALISE_LAG = 2
 TURN_QN_LAG = 3
 PRODUCT_2_LAG = 4
 FINISH_LAG = 5
+PREPARE_WQ_A_STEP = 0
+PREPARE_WQ_B_STEP = 1
 
 FLOPS = 2 * BATCH * SEQ * (DIM * Q_LORA + Q_LORA * HEADS * (NOPE + ROPE))
 
@@ -58,10 +60,14 @@ def tile_mla_pa_t_kernel(
         ps_words = ctx.enter_context(tc.psum_pool(name="ps_words", bufs=2))
         ps_ql = ctx.enter_context(tc.psum_pool(name="ps_ql", bufs=3))
         ps_qnt = ctx.enter_context(tc.psum_pool(name="ps_qnt", bufs=1))
-        ps_q = ctx.enter_context(tc.psum_pool(name="ps_q", bufs=2))
+        ps_nope = ctx.enter_context(tc.psum_pool(name="ps_nope", bufs=1))
+        ps_rope = ctx.enter_context(tc.psum_pool(name="ps_rope", bufs=1))
 
-        wa_rows = keep.tile([P, PACK, DIM], BF16)
-        nc.sync.dma_start(out=wa_rows[:], in_=wq_a.rearrange("(r t) k -> r t k", t=PACK))
+        def copy_out(i, out, in_):
+            if i % 2 == 0:
+                nc.scalar.copy(out=out, in_=in_)
+            else:
+                nc.vector.tensor_copy(out=out, in_=in_)
 
         x_rows = []
         for r in range(ROUNDS):
@@ -73,6 +79,12 @@ def tile_mla_pa_t_kernel(
             nc.sync.dma_start(out=x_rows[r][:], in_=x_view[b, :, s0 : s0 + ROUND_TILES, :])
 
         load_x(0)
+
+        wa_rows = keep.tile([P, PACK, DIM], BF16)
+        wa_view = wq_a.rearrange("(r t) k -> r t k", t=PACK)
+        for t in range(0, PACK, 2):
+            nc.sync.dma_start(out=wa_rows[:, t : t + 2, :], in_=wa_view[:, t : t + 2, :])
+
         load_x(1)
 
         wb_rows = keep.tile([P, 3, Q_LORA], BF16)
@@ -86,10 +98,11 @@ def tile_mla_pa_t_kernel(
         for r in range(2, ROUNDS):
             load_x(r)
 
+        gain_row = keep.tile([P, Q_LORA], BF16)
+        nc.gpsimd.memset(gain_row[:], 0.0)
+        nc.scalar.dma_start(out=gain_row[0:1, :], in_=q_norm_w.rearrange("(o n) -> o n", o=1))
         cos_rows = keep.tile([P, SEQ_TILES, ROPE // 2], BF16)
         sin_rows = keep.tile([P, SEQ_TILES, ROPE // 2], BF16)
-        gain_rows = keep.tile([P, Q_LORA], BF16)
-        nc.scalar.dma_start(out=gain_rows[:], in_=q_norm_w.partition_broadcast(P))
         nc.scalar.dma_start(
             out=cos_rows[:], in_=freqs_cos.rearrange("(p s) j -> p s j", s=SEQ_TILES)
         )
@@ -101,75 +114,92 @@ def tile_mla_pa_t_kernel(
         make_identity(nc, ident_f32[:])
         ident_bf16 = keep.tile([P, P], BF16)
         make_identity(nc, ident_bf16[:])
+        ones = keep.tile([P, P], BF16)
+        nc.gpsimd.memset(ones[:], 1.0)
 
         warm = keep.tile([P, 1], F32)
         nc.scalar.activation(out=warm[:], in_=ident_f32[:, 0:1], func=ACT.Sqrt)
 
-        gain = keep.tile([P, Q_LORA], F32)
-        nc.gpsimd.tensor_copy(
-            out=gain[:].rearrange("p (t r) -> p t r", t=PACK),
-            in_=gain_rows[:].rearrange("p (r t) -> p t r", t=PACK),
-        )
-
-        rot = keep.tile([P, SEQ_TILES, 2, ROPE], F32)
-        rot_pairs = rot[:].rearrange("p s c (j e) -> p s c j e", e=2)
-        nc.gpsimd.tensor_copy(out=rot_pairs[:, :, 0, :, 0], in_=cos_rows[:])
-        nc.gpsimd.tensor_copy(out=rot_pairs[:, :, 0, :, 1], in_=cos_rows[:])
-        nc.gpsimd.tensor_scalar_mul(out=rot_pairs[:, :, 1, :, 0], in0=sin_rows[:], scalar1=-1.0)
-        nc.gpsimd.tensor_copy(out=rot_pairs[:, :, 1, :, 1], in_=sin_rows[:])
+        rot = keep.tile([P, SEQ_TILES, 2, HEADS, ROPE], F32)
+        rot_pairs = rot[:].rearrange("p s c h (j e) -> p s c h j e", e=2)
+        both_heads = [P, SEQ_TILES, HEADS, ROPE // 2]
+        cos_heads = cos_rows[:].unsqueeze(2).to_broadcast(both_heads)
+        sin_heads = sin_rows[:].unsqueeze(2).to_broadcast(both_heads)
+        nc.gpsimd.tensor_copy(out=rot_pairs[:, :, 0, :, :, 0], in_=cos_heads)
+        nc.gpsimd.tensor_copy(out=rot_pairs[:, :, 0, :, :, 1], in_=cos_heads)
+        nc.gpsimd.tensor_scalar_mul(out=rot_pairs[:, :, 1, :, :, 0], in0=sin_heads, scalar1=-1.0)
+        nc.gpsimd.tensor_copy(out=rot_pairs[:, :, 1, :, :, 1], in_=sin_heads)
 
         def turn_words(bank, word_blocks):
             for i, block in enumerate(word_blocks):
                 nc.tensor.transpose(bank[:, i, :], block, ident_f32[:])
 
-        wa_grouped = keep.tile([P, PASSES_1 * Q_LORA * PACK], BF16, align_bytes=64)
-        wa_grouped_words = wa_grouped[:].bitcast(F32).rearrange(
-            "p (g n u) -> p g n u", g=PASSES_1, u=2
-        )
-        for t in range(PACK):
-            words = wa_rows[:, t, :].bitcast(F32)
-            bank = ps_words.tile([P, WORD_BLOCKS, P], F32, tag="words")
-            turn_words(bank, [words[:, i * P : (i + 1) * P] for i in range(WORD_BLOCKS)])
-            nc.vector.tensor_copy(
-                out=wa_grouped_words[:, :, t * P : (t + 1) * P, :],
-                in_=bank[:].rearrange("p (g u) r -> p g r u", u=2),
+        wa_codes = keep.tile([P, PASSES_1, Q_LORA], U32, align_bytes=64)
+        wa_scales = keep.tile([P, PASSES_1, Q_LORA], U8, align_bytes=64)
+        gain = keep.tile([P, Q_LORA], F32)
+
+        def prepare_wq_a():
+            grouped = keep.tile([P, PASSES_1 * Q_LORA * PACK], BF16, align_bytes=64, name="wa_grouped")
+            grouped_words = grouped[:].bitcast(F32).rearrange(
+                "p (g n u) -> p g n u", g=PASSES_1, u=2
             )
-        wa_codes = keep.tile([P, PASSES_1 * Q_LORA], U32, align_bytes=64)
-        wa_scales = keep.tile([P, PASSES_1 * Q_LORA], U8, align_bytes=64)
-        nc.vector.quantize_mx(
-            out=wa_codes[:].bitcast(FP8X4), scales=wa_scales[:], in_=wa_grouped[:]
-        )
+            for t in range(PACK):
+                words = wa_rows[:, t, :].bitcast(F32)
+                bank = ps_words.tile([P, WORD_BLOCKS, P], F32, tag="words")
+                turn_words(bank, [words[:, i * P : (i + 1) * P] for i in range(WORD_BLOCKS)])
+                copy_out(
+                    t,
+                    out=grouped_words[:, :, t * P : (t + 1) * P, :],
+                    in_=bank[:].rearrange("p (g u) r -> p g r u", u=2),
+                )
+                if t % 2 == 1:
+                    cols = slice((t - 1) * P, (t + 1) * P)
+                    for g in range(PASSES_1):
+                        first = (g * Q_LORA + (t - 1) * P) * PACK
+                        nc.vector.quantize_mx(
+                            out=wa_codes[:, g, cols].bitcast(FP8X4),
+                            scales=wa_scales[:, g, cols],
+                            in_=grouped[:, first : first + 2 * P * PACK],
+                        )
+            spread = ps_ql.tile([P, Q_LORA], F32, tag="ql")
+            nc.tensor.matmul(out=spread[:], lhsT=ones[:], rhs=gain_row[:], start=True, stop=True)
+            nc.scalar.copy(
+                out=gain[:].rearrange("p (t r) -> p t r", t=PACK),
+                in_=spread[:].rearrange("p (r t) -> p t r", t=PACK),
+            )
 
-        wb_grouped = keep.tile([P, Q_COLS * PACK], BF16, align_bytes=64)
-        wb_grouped_words = wb_grouped[:].bitcast(F32).rearrange("p (n u) -> p n u", u=2)
-
-        def wb_word_blocks(c):
-            words = wb_rows[:, c, :].bitcast(F32).rearrange("r (p u) -> r u p", u=2)
-            return [words[:, u, :] for u in range(2)]
-
-        bank = ps_words.tile([P, 2 * HEADS, P], F32, tag="words")
-        turn_words(bank, wb_word_blocks(0) + wb_word_blocks(1))
-        nc.vector.tensor_copy(
-            out=wb_grouped_words[:, 0:NOPE_COLS, :].rearrange("p (c r) u -> p c r u", c=HEADS),
-            in_=bank[:].rearrange("p (c u) r -> p c r u", u=2),
-        )
-        bank = ps_words.tile([P, 2, P], F32, tag="words")
-        turn_words(bank, wb_word_blocks(HEADS))
-        nc.vector.tensor_copy(
-            out=wb_grouped_words[:, NOPE_COLS : NOPE_COLS + ROPE_COLS, :],
-            in_=bank[:].rearrange("p u r -> p r u"),
-        )
-        swapped = wb_grouped_words[:, NOPE_COLS + ROPE_COLS : Q_COLS, :].rearrange(
-            "p (m e) u -> p m e u", e=2
-        )
-        pairs = bank[:].rearrange("p u (m e) -> p m e u", e=2)
-        for e in range(2):
-            nc.vector.tensor_copy(out=swapped[:, :, 1 - e, :], in_=pairs[:, :, e, :])
         wb_codes = keep.tile([P, Q_COLS], U32, align_bytes=64)
         wb_scales = keep.tile([P, Q_COLS], U8, align_bytes=64)
-        nc.vector.quantize_mx(
-            out=wb_codes[:].bitcast(FP8X4), scales=wb_scales[:], in_=wb_grouped[:]
-        )
+
+        def prepare_wq_b():
+            grouped = keep.tile([P, Q_COLS * PACK], BF16, align_bytes=64, name="wb_grouped")
+            grouped_words = grouped[:].bitcast(F32).rearrange("p (n u) -> p n u", u=2)
+
+            def word_blocks(c):
+                words = wb_rows[:, c, :].bitcast(F32).rearrange("r (p u) -> r u p", u=2)
+                return [words[:, u, :] for u in range(2)]
+
+            bank = ps_words.tile([P, 2 * HEADS, P], F32, tag="words")
+            turn_words(bank, word_blocks(0) + word_blocks(1))
+            nc.scalar.copy(
+                out=grouped_words[:, 0:NOPE_COLS, :].rearrange("p (c r) u -> p c r u", c=HEADS),
+                in_=bank[:].rearrange("p (c u) r -> p c r u", u=2),
+            )
+            bank = ps_words.tile([P, 2, P], F32, tag="words")
+            turn_words(bank, word_blocks(HEADS))
+            nc.vector.tensor_copy(
+                out=grouped_words[:, NOPE_COLS : NOPE_COLS + ROPE_COLS, :],
+                in_=bank[:].rearrange("p u r -> p r u"),
+            )
+            swapped = grouped_words[:, NOPE_COLS + ROPE_COLS : Q_COLS, :].rearrange(
+                "p (m e) u -> p m e u", e=2
+            )
+            pairs = bank[:].rearrange("p u (m e) -> p m e u", e=2)
+            for e in range(2):
+                nc.vector.tensor_copy(out=swapped[:, :, 1 - e, :], in_=pairs[:, :, e, :])
+            nc.vector.quantize_mx(
+                out=wb_codes[:].bitcast(FP8X4), scales=wb_scales[:], in_=grouped[:]
+            )
 
         x_grouped, x_mx, ql_banks, rms_of = {}, {}, {}, {}
         qn_of, qn_grouped, qn_mx, q_banks = {}, {}, {}, {}
@@ -183,8 +213,8 @@ def tile_mla_pa_t_kernel(
                 words = x_rows[r][:, j, :].bitcast(F32)
                 bank = ps_words.tile([P, WORD_BLOCKS, P], F32, tag="words")
                 turn_words(bank, [words[:, i * P : (i + 1) * P] for i in range(WORD_BLOCKS)])
-                nc.scalar.copy(
-                    out=grouped_words[:, j], in_=bank[:].rearrange("p (g u) r -> p g r u", u=2)
+                copy_out(
+                    j, out=grouped_words[:, j], in_=bank[:].rearrange("p (g u) r -> p g r u", u=2)
                 )
             x_grouped[r] = grouped
 
@@ -204,13 +234,12 @@ def tile_mla_pa_t_kernel(
                 ql = ps_ql.tile([P, Q_LORA], F32, tag="ql")
                 for g in range(PASSES_1):
                     tok = slice((j * PASSES_1 + g) * P, (j * PASSES_1 + g + 1) * P)
-                    col = slice(g * Q_LORA, (g + 1) * Q_LORA)
                     nc.tensor.matmul_mx(
                         out=ql[:],
                         lhsT=codes[:, tok].bitcast(FP8X4),
                         lhsT_scale=scales[:, tok],
-                        rhs=wa_codes[:, col].bitcast(FP8X4),
-                        rhs_scale=wa_scales[:, col],
+                        rhs=wa_codes[:, g, :].bitcast(FP8X4),
+                        rhs_scale=wa_scales[:, g, :],
                         start=(g == 0),
                         stop=(g == PASSES_1 - 1),
                     )
@@ -264,37 +293,43 @@ def tile_mla_pa_t_kernel(
 
         def product_2(r):
             codes, scales = qn_mx[r]
-            q_banks[r] = []
+            nope_bank = ps_nope.tile([P, ROUND_TILES, NOPE_COLS], F32, tag="nope_bank")
+            rope_bank = ps_rope.tile([P, ROUND_TILES, 2 * ROPE_COLS], F32, tag="rope_bank")
             for j in range(ROUND_TILES):
                 tok = slice(j * P, (j + 1) * P)
-                q = ps_q.tile([P, Q_COLS], F32, tag="q")
-                nc.tensor.matmul_mx(
-                    out=q[:],
-                    lhsT=codes[:, tok].bitcast(FP8X4),
-                    lhsT_scale=scales[:, tok],
-                    rhs=wb_codes[:].bitcast(FP8X4),
-                    rhs_scale=wb_scales[:],
-                    start=True,
-                    stop=True,
-                )
-                q_banks[r].append(q)
+                for bank, cols in (
+                    (nope_bank, slice(0, NOPE_COLS)),
+                    (rope_bank, slice(NOPE_COLS, Q_COLS)),
+                ):
+                    nc.tensor.matmul_mx(
+                        out=bank[:, j, :],
+                        lhsT=codes[:, tok].bitcast(FP8X4),
+                        lhsT_scale=scales[:, tok],
+                        rhs=wb_codes[:, cols].bitcast(FP8X4),
+                        rhs_scale=wb_scales[:, cols],
+                        start=True,
+                        stop=True,
+                    )
+            q_banks[r] = (nope_bank, rope_bank)
 
         def finish(r):
             b, s0 = r // ROUNDS_PER_BATCH, (r % ROUNDS_PER_BATCH) * ROUND_TILES
+            nope_bank, rope_bank = q_banks[r]
             nope = ring.tile([P, ROUND_TILES, NOPE_COLS], F32, tag="nope")
-            terms = ring.tile([P, ROUND_TILES, 2, ROPE_COLS], F32, tag="terms")
+            nc.scalar.copy(out=nope[:], in_=nope_bank[:])
+            terms = ring.tile([P, ROUND_TILES, 2 * ROPE_COLS], F32, tag="terms")
+            nc.vector.tensor_tensor(
+                out=terms[:],
+                in0=rope_bank[:],
+                in1=rot[:, s0 : s0 + ROUND_TILES].rearrange("p s c h d -> p s (c h d)"),
+                op=ALU.mult,
+            )
             rope = ring.tile([P, ROUND_TILES, ROPE_COLS], F32, tag="rope")
-            for j in range(ROUND_TILES):
-                q = q_banks[r][j]
-                nc.vector.tensor_copy(out=nope[:, j, :], in_=q[:, 0:NOPE_COLS])
-                nc.vector.tensor_tensor(
-                    out=terms[:, j].rearrange("p c (h d) -> p c h d", h=HEADS),
-                    in0=q[:, NOPE_COLS:Q_COLS].rearrange("p (c h d) -> p c h d", c=2, h=HEADS),
-                    in1=rot[:, s0 + j].unsqueeze(2).to_broadcast([P, 2, HEADS, ROPE]),
-                    op=ALU.mult,
-                )
             nc.gpsimd.tensor_tensor(
-                out=rope[:], in0=terms[:, :, 0, :], in1=terms[:, :, 1, :], op=ALU.add
+                out=rope[:],
+                in0=terms[:, :, 0:ROPE_COLS],
+                in1=terms[:, :, ROPE_COLS : 2 * ROPE_COLS],
+                op=ALU.add,
             )
             nc.sync.dma_start(out=nope_view[b, :, s0 : s0 + ROUND_TILES, :], in_=nope[:])
             nc.sync.dma_start(out=rope_view[b, :, s0 : s0 + ROUND_TILES, :], in_=rope[:])
@@ -308,7 +343,11 @@ def tile_mla_pa_t_kernel(
             run(normalise, i - NORMALISE_LAG)
             run(turn_x, i)
             run(turn_qn, i - TURN_QN_LAG)
-            run(quantise_x, i)
             run(quantise_qn, i - TURN_QN_LAG)
+            run(quantise_x, i)
+            if i == PREPARE_WQ_A_STEP:
+                prepare_wq_a()
+            if i == PREPARE_WQ_B_STEP:
+                prepare_wq_b()
             run(product_1, i - PRODUCT_1_LAG)
             run(product_2, i - PRODUCT_2_LAG)

@@ -52,8 +52,6 @@ def tile_mla_pa_t_kernel(
     rope_view = out_1.rearrange("b (p s) h d -> b p s (h d)", s=SEQ_TILES)
 
     with ExitStack() as ctx:
-        ctx.enter_context(tc.manual_schedule())
-
         keep = ctx.enter_context(tc.tile_pool(name="keep", bufs=1))
         stage = ctx.enter_context(tc.tile_pool(name="stage", bufs=2))
         ring = ctx.enter_context(tc.tile_pool(name="ring", bufs=3))

@@ -37,7 +37,8 @@ TURN_QN_LAG = 3
 PRODUCT_2_LAG = 4
 FINISH_LAG = 5
 PREPARE_WQ_A_STEP = 0
-PREPARE_WQ_B_STEP = 1
+PREPARE_ROTATION_STEP = 1
+PREPARE_WQ_B_STEP = 2
 
 FLOPS = 2 * BATCH * SEQ * (DIM * Q_LORA + Q_LORA * HEADS * (NOPE + ROPE))
 
@@ -52,6 +53,8 @@ def tile_mla_pa_t_kernel(
     rope_view = out_1.rearrange("b (p s) h d -> b p s (h d)", s=SEQ_TILES)
 
     with ExitStack() as ctx:
+        ctx.enter_context(tc.manual_schedule())
+
         keep = ctx.enter_context(tc.tile_pool(name="keep", bufs=1))
         stage = ctx.enter_context(tc.tile_pool(name="stage", bufs=2))
         ring = ctx.enter_context(tc.tile_pool(name="ring", bufs=3))
@@ -116,17 +119,27 @@ def tile_mla_pa_t_kernel(
         nc.gpsimd.memset(ones[:], 1.0)
 
         warm = keep.tile([P, 1], F32)
-        nc.scalar.activation(out=warm[:], in_=ident_f32[:, 0:1], func=ACT.Sqrt)
+        nc.scalar.activation(out=warm[:], in_=ones[:, 0:1], func=ACT.Abs_reciprocal_sqrt)
 
-        rot = keep.tile([P, SEQ_TILES, 2, HEADS, ROPE], F32)
-        rot_pairs = rot[:].rearrange("p s c h (j e) -> p s c h j e", e=2)
-        both_heads = [P, SEQ_TILES, HEADS, ROPE // 2]
-        cos_heads = cos_rows[:].unsqueeze(2).to_broadcast(both_heads)
-        sin_heads = sin_rows[:].unsqueeze(2).to_broadcast(both_heads)
-        nc.gpsimd.tensor_copy(out=rot_pairs[:, :, 0, :, :, 0], in_=cos_heads)
-        nc.gpsimd.tensor_copy(out=rot_pairs[:, :, 0, :, :, 1], in_=cos_heads)
-        nc.gpsimd.tensor_scalar_mul(out=rot_pairs[:, :, 1, :, :, 0], in0=sin_heads, scalar1=-1.0)
-        nc.gpsimd.tensor_copy(out=rot_pairs[:, :, 1, :, :, 1], in_=sin_heads)
+        rot = keep.tile([P, SEQ_TILES, 2, ROPE], F32)
+
+        def prepare_rotation():
+            pairs = rot[:].rearrange("p s c (j e) -> p s c j e", e=2)
+            nc.vector.tensor_copy(
+                out=pairs[:, :, 0, :, :],
+                in_=cos_rows[:].unsqueeze(3).to_broadcast([P, SEQ_TILES, ROPE // 2, 2]),
+            )
+            nc.vector.tensor_scalar_mul(out=pairs[:, :, 1, :, 0], in0=sin_rows[:], scalar1=-1.0)
+            nc.vector.tensor_copy(out=pairs[:, :, 1, :, 1], in_=sin_rows[:])
+
+        def idle_bank(i, blocks):
+            pool, tag = (
+                (ps_qnt, "qnt"),
+                (ps_nope, "nope_bank"),
+                (ps_rope, "rope_bank"),
+                (ps_ql, "ql"),
+            )[i]
+            return pool.tile([P, blocks, P], F32, tag=tag, name="weight_bank")
 
         def turn_words(bank, word_blocks):
             for i, block in enumerate(word_blocks):
@@ -143,7 +156,7 @@ def tile_mla_pa_t_kernel(
             )
             for t in range(PACK):
                 words = wa_rows[:, t, :].bitcast(F32)
-                bank = ps_words.tile([P, WORD_BLOCKS, P], F32, tag="words")
+                bank = idle_bank(t, WORD_BLOCKS)
                 turn_words(bank, [words[:, i * P : (i + 1) * P] for i in range(WORD_BLOCKS)])
                 copy_out(
                     t,
@@ -177,15 +190,15 @@ def tile_mla_pa_t_kernel(
                 words = wb_rows[:, c, :].bitcast(F32).rearrange("r (p u) -> r u p", u=2)
                 return [words[:, u, :] for u in range(2)]
 
-            bank = ps_words.tile([P, 2 * HEADS, P], F32, tag="words")
+            bank = idle_bank(1, 2 * HEADS)
             turn_words(bank, word_blocks(0) + word_blocks(1))
             nc.scalar.copy(
                 out=grouped_words[:, 0:NOPE_COLS, :].rearrange("p (c r) u -> p c r u", c=HEADS),
                 in_=bank[:].rearrange("p (c u) r -> p c r u", u=2),
             )
-            bank = ps_words.tile([P, 2, P], F32, tag="words")
+            bank = idle_bank(2, 2)
             turn_words(bank, word_blocks(HEADS))
-            nc.vector.tensor_copy(
+            nc.scalar.copy(
                 out=grouped_words[:, NOPE_COLS : NOPE_COLS + ROPE_COLS, :],
                 in_=bank[:].rearrange("p u r -> p r u"),
             )
@@ -194,12 +207,12 @@ def tile_mla_pa_t_kernel(
             )
             pairs = bank[:].rearrange("p u (m e) -> p m e u", e=2)
             for e in range(2):
-                nc.vector.tensor_copy(out=swapped[:, :, 1 - e, :], in_=pairs[:, :, e, :])
+                nc.scalar.copy(out=swapped[:, :, 1 - e, :], in_=pairs[:, :, e, :])
             nc.vector.quantize_mx(
                 out=wb_codes[:].bitcast(FP8X4), scales=wb_scales[:], in_=grouped[:]
             )
 
-        x_grouped, x_mx, ql_banks, rms_of = {}, {}, {}, {}
+        x_grouped, x_mx, ql_banks, rstd_of = {}, {}, {}, {}
         qn_of, qn_grouped, qn_mx, q_banks = {}, {}, {}, {}
 
         def turn_x(r):
@@ -246,15 +259,18 @@ def tile_mla_pa_t_kernel(
                     out=squares[:], in_=ql[:], func=ACT.Square, accum_out=sum_sq[:, j : j + 1]
                 )
                 ql_banks[r].append(ql)
-            rms = ring.tile([P, ROUND_TILES], F32, tag="rms")
+            rstd = ring.tile([P, ROUND_TILES], F32, tag="rstd")
             nc.scalar.activation(
-                out=rms[:], in_=sum_sq[:], func=ACT.Sqrt, bias=EPS, scale=1.0 / Q_LORA
+                out=rstd[:],
+                in_=sum_sq[:],
+                func=ACT.Abs_reciprocal_sqrt,
+                bias=EPS,
+                scale=1.0 / Q_LORA,
             )
-            rms_of[r] = rms
+            rstd_of[r] = rstd
 
         def normalise(r):
-            rstd = ring.tile([P, ROUND_TILES], F32, tag="rstd")
-            nc.vector.reciprocal(out=rstd[:], in_=rms_of[r][:])
+            rstd = rstd_of[r]
             qn = ring.tile([P, ROUND_TILES, Q_LORA], BF16, tag="qn")
             for j in range(ROUND_TILES):
                 nc.vector.scalar_tensor_tensor(
@@ -317,9 +333,12 @@ def tile_mla_pa_t_kernel(
             nc.scalar.copy(out=nope[:], in_=nope_bank[:])
             terms = ring.tile([P, ROUND_TILES, 2 * ROPE_COLS], F32, tag="terms")
             nc.vector.tensor_tensor(
-                out=terms[:],
-                in0=rope_bank[:],
-                in1=rot[:, s0 : s0 + ROUND_TILES].rearrange("p s c h d -> p s (c h d)"),
+                out=terms[:].rearrange("p j (c h d) -> p (j c) h d", c=2, h=HEADS),
+                in0=rope_bank[:].rearrange("p j (c h d) -> p (j c) h d", c=2, h=HEADS),
+                in1=rot[:, s0 : s0 + ROUND_TILES]
+                .rearrange("p s c d -> p (s c) d")
+                .unsqueeze(2)
+                .to_broadcast([P, 2 * ROUND_TILES, HEADS, ROPE]),
                 op=ALU.mult,
             )
             rope = ring.tile([P, ROUND_TILES, ROPE_COLS], F32, tag="rope")
@@ -345,6 +364,8 @@ def tile_mla_pa_t_kernel(
             run(quantise_x, i)
             if i == PREPARE_WQ_A_STEP:
                 prepare_wq_a()
+            if i == PREPARE_ROTATION_STEP:
+                prepare_rotation()
             if i == PREPARE_WQ_B_STEP:
                 prepare_wq_b()
             run(product_1, i - PRODUCT_1_LAG)

@@ -56,7 +56,7 @@ def tile_mla_pa_t_kernel(
         ctx.enter_context(tc.manual_schedule())
 
         keep = ctx.enter_context(tc.tile_pool(name="keep", bufs=1))
-        stage = ctx.enter_context(tc.tile_pool(name="stage", bufs=2))
+        pair = ctx.enter_context(tc.tile_pool(name="pair", bufs=2))
         ring = ctx.enter_context(tc.tile_pool(name="ring", bufs=3))
         ps_words = ctx.enter_context(tc.psum_pool(name="ps_words", bufs=2))
         ps_ql = ctx.enter_context(tc.psum_pool(name="ps_ql", bufs=3))
@@ -64,20 +64,20 @@ def tile_mla_pa_t_kernel(
         ps_nope = ctx.enter_context(tc.psum_pool(name="ps_nope", bufs=1))
         ps_rope = ctx.enter_context(tc.psum_pool(name="ps_rope", bufs=1))
 
-        def copy_out(i, out, in_):
-            if i % 2 == 0:
+        def copy_out(index, out, in_):
+            if index % 2 == 0:
                 nc.scalar.copy(out=out, in_=in_)
             else:
                 nc.vector.tensor_copy(out=out, in_=in_)
 
         x_rows = []
-        for r in range(ROUNDS):
-            x_round = keep.tile([P, ROUND_TILES, DIM], BF16, name="x_round%d" % r)
+        for rnd in range(ROUNDS):
+            x_round = keep.tile([P, ROUND_TILES, DIM], BF16, name="x_round%d" % rnd)
             x_rows.append(x_round)
 
-        def load_x(r):
-            b, s0 = r // ROUNDS_PER_BATCH, (r % ROUNDS_PER_BATCH) * ROUND_TILES
-            nc.sync.dma_start(out=x_rows[r][:], in_=x_view[b, :, s0 : s0 + ROUND_TILES, :])
+        def load_x(rnd):
+            b, s0 = rnd // ROUNDS_PER_BATCH, (rnd % ROUNDS_PER_BATCH) * ROUND_TILES
+            nc.sync.dma_start(out=x_rows[rnd][:], in_=x_view[b, :, s0 : s0 + ROUND_TILES, :])
 
         load_x(0)
 
@@ -88,7 +88,7 @@ def tile_mla_pa_t_kernel(
 
         load_x(1)
 
-        wb_rows = keep.tile([P, 3, Q_LORA], BF16)
+        wb_rows = keep.tile([P, HEADS + 1, Q_LORA], BF16)
         wb_heads = wq_b.rearrange("(h d) k -> d h k", h=HEADS)
         nc.sync.dma_start(out=wb_rows[:, 0:HEADS, :], in_=wb_heads[0:NOPE, :, :])
         for h in range(HEADS):
@@ -96,8 +96,8 @@ def tile_mla_pa_t_kernel(
                 out=wb_rows[h * ROPE : (h + 1) * ROPE, HEADS, :],
                 in_=wb_heads[NOPE : NOPE + ROPE, h, :],
             )
-        for r in range(2, ROUNDS):
-            load_x(r)
+        for rnd in range(2, ROUNDS):
+            load_x(rnd)
 
         gain_row = keep.tile([P, Q_LORA], BF16)
         nc.gpsimd.memset(gain_row[:], 0.0)
@@ -105,10 +105,10 @@ def tile_mla_pa_t_kernel(
         cos_rows = keep.tile([P, SEQ_TILES, ROPE // 2], BF16)
         sin_rows = keep.tile([P, SEQ_TILES, ROPE // 2], BF16)
         nc.scalar.dma_start(
-            out=cos_rows[:], in_=freqs_cos.rearrange("(p s) j -> p s j", s=SEQ_TILES)
+            out=cos_rows[:], in_=freqs_cos.rearrange("(p s) f -> p s f", s=SEQ_TILES)
         )
         nc.scalar.dma_start(
-            out=sin_rows[:], in_=freqs_sin.rearrange("(p s) j -> p s j", s=SEQ_TILES)
+            out=sin_rows[:], in_=freqs_sin.rearrange("(p s) f -> p s f", s=SEQ_TILES)
         )
 
         ident_f32 = keep.tile([P, P], F32)
@@ -124,26 +124,31 @@ def tile_mla_pa_t_kernel(
         rot = keep.tile([P, SEQ_TILES, 2, ROPE], F32)
 
         def prepare_rotation():
-            pairs = rot[:].rearrange("p s c (j e) -> p s c j e", e=2)
+            rot_pairs = rot[:].rearrange("p s c (f e) -> p s c f e", e=2)
             nc.vector.tensor_copy(
-                out=pairs[:, :, 0, :, :],
+                out=rot_pairs[:, :, 0, :, :],
                 in_=cos_rows[:].unsqueeze(3).to_broadcast([P, SEQ_TILES, ROPE // 2, 2]),
             )
-            nc.vector.tensor_scalar_mul(out=pairs[:, :, 1, :, 0], in0=sin_rows[:], scalar1=-1.0)
-            nc.vector.tensor_copy(out=pairs[:, :, 1, :, 1], in_=sin_rows[:])
+            nc.vector.tensor_scalar_mul(
+                out=rot_pairs[:, :, 1, :, 0], in0=sin_rows[:], scalar1=-1.0
+            )
+            nc.vector.tensor_copy(out=rot_pairs[:, :, 1, :, 1], in_=sin_rows[:])
 
-        def idle_bank(i, blocks):
+        def idle_bank(which, blocks):
             pool, tag = (
                 (ps_qnt, "qnt"),
                 (ps_nope, "nope_bank"),
                 (ps_rope, "rope_bank"),
                 (ps_ql, "ql"),
-            )[i]
+            )[which]
             return pool.tile([P, blocks, P], F32, tag=tag, name="weight_bank")
 
         def turn_words(bank, word_blocks):
-            for i, block in enumerate(word_blocks):
-                nc.tensor.transpose(bank[:, i, :], block, ident_f32[:])
+            for slot, block in enumerate(word_blocks):
+                nc.tensor.transpose(bank[:, slot, :], block, ident_f32[:])
+
+        def blocks_of_row_words(words):
+            return [words[:, slot * P : (slot + 1) * P] for slot in range(WORD_BLOCKS)]
 
         wa_codes = keep.tile([P, PASSES_1, Q_LORA], U32, align_bytes=64)
         wa_scales = keep.tile([P, PASSES_1, Q_LORA], U8, align_bytes=64)
@@ -155,9 +160,8 @@ def tile_mla_pa_t_kernel(
                 "p (g n u) -> p g n u", g=PASSES_1, u=2
             )
             for t in range(PACK):
-                words = wa_rows[:, t, :].bitcast(F32)
                 bank = idle_bank(t, WORD_BLOCKS)
-                turn_words(bank, [words[:, i * P : (i + 1) * P] for i in range(WORD_BLOCKS)])
+                turn_words(bank, blocks_of_row_words(wa_rows[:, t, :].bitcast(F32)))
                 copy_out(
                     t,
                     out=grouped_words[:, :, t * P : (t + 1) * P, :],
@@ -186,18 +190,18 @@ def tile_mla_pa_t_kernel(
             grouped = keep.tile([P, Q_COLS * PACK], BF16, align_bytes=64, name="wb_grouped")
             grouped_words = grouped[:].bitcast(F32).rearrange("p (n u) -> p n u", u=2)
 
-            def word_blocks(c):
-                words = wb_rows[:, c, :].bitcast(F32).rearrange("r (p u) -> r u p", u=2)
+            def every_second_word(i):
+                words = wb_rows[:, i, :].bitcast(F32).rearrange("r (p u) -> r u p", u=2)
                 return [words[:, u, :] for u in range(2)]
 
             bank = idle_bank(1, 2 * HEADS)
-            turn_words(bank, word_blocks(0) + word_blocks(1))
+            turn_words(bank, every_second_word(0) + every_second_word(1))
             nc.scalar.copy(
-                out=grouped_words[:, 0:NOPE_COLS, :].rearrange("p (c r) u -> p c r u", c=HEADS),
-                in_=bank[:].rearrange("p (c u) r -> p c r u", u=2),
+                out=grouped_words[:, 0:NOPE_COLS, :].rearrange("p (i r) u -> p i r u", i=HEADS),
+                in_=bank[:].rearrange("p (i u) r -> p i r u", u=2),
             )
             bank = idle_bank(2, 2)
-            turn_words(bank, word_blocks(HEADS))
+            turn_words(bank, every_second_word(HEADS))
             nc.scalar.copy(
                 out=grouped_words[:, NOPE_COLS : NOPE_COLS + ROPE_COLS, :],
                 in_=bank[:].rearrange("p u r -> p r u"),
@@ -205,9 +209,9 @@ def tile_mla_pa_t_kernel(
             swapped = grouped_words[:, NOPE_COLS + ROPE_COLS : Q_COLS, :].rearrange(
                 "p (m e) u -> p m e u", e=2
             )
-            pairs = bank[:].rearrange("p u (m e) -> p m e u", e=2)
+            row_pairs = bank[:].rearrange("p u (m e) -> p m e u", e=2)
             for e in range(2):
-                nc.scalar.copy(out=swapped[:, :, 1 - e, :], in_=pairs[:, :, e, :])
+                nc.scalar.copy(out=swapped[:, :, 1 - e, :], in_=row_pairs[:, :, e, :])
             nc.vector.quantize_mx(
                 out=wb_codes[:].bitcast(FP8X4), scales=wb_scales[:], in_=grouped[:]
             )
@@ -215,32 +219,31 @@ def tile_mla_pa_t_kernel(
         x_grouped, x_mx, ql_banks, rstd_of = {}, {}, {}, {}
         qn_of, qn_grouped, qn_mx, q_banks = {}, {}, {}, {}
 
-        def turn_x(r):
-            grouped = stage.tile([P, ROUND_TILES * DIM], BF16, align_bytes=64, tag="x_grouped")
+        def turn_x(rnd):
+            grouped = pair.tile([P, ROUND_TILES * DIM], BF16, align_bytes=64, tag="x_grouped")
             grouped_words = grouped[:].bitcast(F32).rearrange(
                 "p (j g r u) -> p j g r u", j=ROUND_TILES, g=PASSES_1, u=2
             )
             for j in range(ROUND_TILES):
-                words = x_rows[r][:, j, :].bitcast(F32)
                 bank = ps_words.tile([P, WORD_BLOCKS, P], F32, tag="words")
-                turn_words(bank, [words[:, i * P : (i + 1) * P] for i in range(WORD_BLOCKS)])
+                turn_words(bank, blocks_of_row_words(x_rows[rnd][:, j, :].bitcast(F32)))
                 copy_out(
                     j, out=grouped_words[:, j], in_=bank[:].rearrange("p (g u) r -> p g r u", u=2)
                 )
-            x_grouped[r] = grouped
+            x_grouped[rnd] = grouped
 
-        def quantise_x(r):
+        def quantise_x(rnd):
             codes = ring.tile([P, ROUND_TILES * PASSES_1 * P], U32, align_bytes=64, tag="x_codes")
             scales = ring.tile([P, ROUND_TILES * PASSES_1 * P], U8, align_bytes=64, tag="x_scales")
             nc.vector.quantize_mx(
-                out=codes[:].bitcast(FP8X4), scales=scales[:], in_=x_grouped[r][:]
+                out=codes[:].bitcast(FP8X4), scales=scales[:], in_=x_grouped[rnd][:]
             )
-            x_mx[r] = (codes, scales)
+            x_mx[rnd] = (codes, scales)
 
-        def product_1(r):
-            codes, scales = x_mx[r]
+        def product_1(rnd):
+            codes, scales = x_mx[rnd]
             sum_sq = ring.tile([P, ROUND_TILES], F32, tag="sum_sq")
-            ql_banks[r] = []
+            ql_banks[rnd] = []
             for j in range(ROUND_TILES):
                 ql = ps_ql.tile([P, Q_LORA], F32, tag="ql")
                 for g in range(PASSES_1):
@@ -254,11 +257,11 @@ def tile_mla_pa_t_kernel(
                         start=(g == 0),
                         stop=(g == PASSES_1 - 1),
                     )
-                squares = stage.tile([P, Q_LORA], BF16, tag="squares")
+                squares = pair.tile([P, Q_LORA], BF16, tag="squares")
                 nc.scalar.activation(
                     out=squares[:], in_=ql[:], func=ACT.Square, accum_out=sum_sq[:, j : j + 1]
                 )
-                ql_banks[r].append(ql)
+                ql_banks[rnd].append(ql)
             rstd = ring.tile([P, ROUND_TILES], F32, tag="rstd")
             nc.scalar.activation(
                 out=rstd[:],
@@ -267,46 +270,46 @@ def tile_mla_pa_t_kernel(
                 bias=EPS,
                 scale=1.0 / Q_LORA,
             )
-            rstd_of[r] = rstd
+            rstd_of[rnd] = rstd
 
-        def normalise(r):
-            rstd = rstd_of[r]
+        def normalise(rnd):
+            rstd = rstd_of[rnd]
             qn = ring.tile([P, ROUND_TILES, Q_LORA], BF16, tag="qn")
             for j in range(ROUND_TILES):
                 nc.vector.scalar_tensor_tensor(
                     out=qn[:, j, :],
-                    in0=ql_banks[r][j][:],
+                    in0=ql_banks[rnd][j][:],
                     scalar=rstd[:, j : j + 1],
                     in1=gain[:],
                     op0=ALU.mult,
                     op1=ALU.mult,
                 )
-            qn_of[r] = qn
+            qn_of[rnd] = qn
 
-        def turn_qn(r):
+        def turn_qn(rnd):
             qnt = ps_qnt.tile([P, ROUND_TILES, PACK, P], BF16, tag="qnt")
             for j in range(ROUND_TILES):
                 for t in range(PACK):
                     nc.tensor.transpose(
-                        qnt[:, j, t, :], qn_of[r][:, j, t * P : (t + 1) * P], ident_bf16[:]
+                        qnt[:, j, t, :], qn_of[rnd][:, j, t * P : (t + 1) * P], ident_bf16[:]
                     )
-            grouped = stage.tile([P, ROUND_TILES * Q_LORA], BF16, align_bytes=64, tag="qn_grouped")
+            grouped = pair.tile([P, ROUND_TILES * Q_LORA], BF16, align_bytes=64, tag="qn_grouped")
             nc.scalar.copy(
                 out=grouped[:].rearrange("p (j r t) -> p j r t", j=ROUND_TILES, t=PACK),
                 in_=qnt[:].rearrange("p j t r -> p j r t"),
             )
-            qn_grouped[r] = grouped
+            qn_grouped[rnd] = grouped
 
-        def quantise_qn(r):
+        def quantise_qn(rnd):
             codes = ring.tile([P, ROUND_TILES * P], U32, align_bytes=64, tag="qn_codes")
             scales = ring.tile([P, ROUND_TILES * P], U8, align_bytes=64, tag="qn_scales")
             nc.vector.quantize_mx(
-                out=codes[:].bitcast(FP8X4), scales=scales[:], in_=qn_grouped[r][:]
+                out=codes[:].bitcast(FP8X4), scales=scales[:], in_=qn_grouped[rnd][:]
             )
-            qn_mx[r] = (codes, scales)
+            qn_mx[rnd] = (codes, scales)
 
-        def product_2(r):
-            codes, scales = qn_mx[r]
+        def product_2(rnd):
+            codes, scales = qn_mx[rnd]
             nope_bank = ps_nope.tile([P, ROUND_TILES, NOPE_COLS], F32, tag="nope_bank")
             rope_bank = ps_rope.tile([P, ROUND_TILES, 2 * ROPE_COLS], F32, tag="rope_bank")
             for j in range(ROUND_TILES):
@@ -324,11 +327,11 @@ def tile_mla_pa_t_kernel(
                         start=True,
                         stop=True,
                     )
-            q_banks[r] = (nope_bank, rope_bank)
+            q_banks[rnd] = (nope_bank, rope_bank)
 
-        def finish(r):
-            b, s0 = r // ROUNDS_PER_BATCH, (r % ROUNDS_PER_BATCH) * ROUND_TILES
-            nope_bank, rope_bank = q_banks[r]
+        def finish(rnd):
+            b, s0 = rnd // ROUNDS_PER_BATCH, (rnd % ROUNDS_PER_BATCH) * ROUND_TILES
+            nope_bank, rope_bank = q_banks[rnd]
             nope = ring.tile([P, ROUND_TILES, NOPE_COLS], F32, tag="nope")
             nc.scalar.copy(out=nope[:], in_=nope_bank[:])
             terms = ring.tile([P, ROUND_TILES, 2 * ROPE_COLS], F32, tag="terms")
@@ -351,22 +354,22 @@ def tile_mla_pa_t_kernel(
             nc.sync.dma_start(out=nope_view[b, :, s0 : s0 + ROUND_TILES, :], in_=nope[:])
             nc.sync.dma_start(out=rope_view[b, :, s0 : s0 + ROUND_TILES, :], in_=rope[:])
 
-        def run(stage_fn, r):
-            if 0 <= r < ROUNDS:
-                stage_fn(r)
+        def run(stage_of_round, rnd):
+            if 0 <= rnd < ROUNDS:
+                stage_of_round(rnd)
 
-        for i in range(ROUNDS + FINISH_LAG):
-            run(finish, i - FINISH_LAG)
-            run(normalise, i - NORMALISE_LAG)
-            run(turn_x, i)
-            run(turn_qn, i - TURN_QN_LAG)
-            run(quantise_qn, i - TURN_QN_LAG)
-            run(quantise_x, i)
-            if i == PREPARE_WQ_A_STEP:
+        for step in range(ROUNDS + FINISH_LAG):
+            run(finish, step - FINISH_LAG)
+            run(normalise, step - NORMALISE_LAG)
+            run(turn_x, step)
+            run(turn_qn, step - TURN_QN_LAG)
+            run(quantise_qn, step - TURN_QN_LAG)
+            run(quantise_x, step)
+            if step == PREPARE_WQ_A_STEP:
                 prepare_wq_a()
-            if i == PREPARE_ROTATION_STEP:
+            if step == PREPARE_ROTATION_STEP:
                 prepare_rotation()
-            if i == PREPARE_WQ_B_STEP:
+            if step == PREPARE_WQ_B_STEP:
                 prepare_wq_b()
-            run(product_1, i - PRODUCT_1_LAG)
-            run(product_2, i - PRODUCT_2_LAG)
+            run(product_1, step - PRODUCT_1_LAG)
+            run(product_2, step - PRODUCT_2_LAG)

from contextlib import ExitStack

import concourse.mybir as mybir
from concourse.masks import make_identity

F32 = mybir.dt.float32
BF16 = mybir.dt.bfloat16
U32 = mybir.dt.uint32
U8 = mybir.dt.uint8
FP8X4 = mybir.dt.float8_e4m3fn_x4
ACT = mybir.ActivationFunctionType
ALU = mybir.AluOpType

P = 128
PACK = 4
K_PASS = P * PACK

BATCH, SEQ, DIM = 4, 1024, 1024
Q_LORA = 512
HEADS, NOPE, ROPE = 2, 128, 64
EPS = 1e-6

SEQ_TILES = SEQ // P
PASSES_1 = DIM // K_PASS
WORD_BLOCKS = DIM // 2 // P
NOPE_COLS = HEADS * NOPE
ROPE_COLS = HEADS * ROPE
Q_COLS = NOPE_COLS + 2 * ROPE_COLS

ROUND_TILES = 2
ROUNDS = BATCH * SEQ_TILES // ROUND_TILES
ROUNDS_PER_BATCH = SEQ_TILES // ROUND_TILES

PRODUCT_1_LAG = 1
NORMALISE_LAG = 2
TURN_QN_LAG = 3
PRODUCT_2_LAG = 4
FINISH_LAG = 5
PREPARE_WQ_A_STEP = 0
PREPARE_ROTATION_STEP = 1
PREPARE_WQ_B_STEP = 2

FLOPS = 2 * BATCH * SEQ * (DIM * Q_LORA + Q_LORA * HEADS * (NOPE + ROPE))


def tile_mla_pa_t_kernel(
    tc, x, freqs_cos, freqs_sin, wq_a, q_norm_w, wq_b, out_0, out_1
):
    nc = tc.nc

    x_view = x.rearrange("b (p s) k -> b p s k", s=SEQ_TILES)
    nope_view = out_0.rearrange("b (p s) h d -> b p s (h d)", s=SEQ_TILES)
    rope_view = out_1.rearrange("b (p s) h d -> b p s (h d)", s=SEQ_TILES)

    with ExitStack() as ctx:
        ctx.enter_context(tc.manual_schedule())

        keep = ctx.enter_context(tc.tile_pool(name="keep", bufs=1))
        pair = ctx.enter_context(tc.tile_pool(name="pair", bufs=2))
        ring = ctx.enter_context(tc.tile_pool(name="ring", bufs=3))
        ps_words = ctx.enter_context(tc.psum_pool(name="ps_words", bufs=2))
        ps_ql = ctx.enter_context(tc.psum_pool(name="ps_ql", bufs=3))
        ps_qnt = ctx.enter_context(tc.psum_pool(name="ps_qnt", bufs=1))
        ps_nope = ctx.enter_context(tc.psum_pool(name="ps_nope", bufs=1))
        ps_rope = ctx.enter_context(tc.psum_pool(name="ps_rope", bufs=1))

        def copy_out(index, out, in_):
            if index % 2 == 0:
                nc.scalar.copy(out=out, in_=in_)
            else:
                nc.vector.tensor_copy(out=out, in_=in_)

        x_rows = []
        for rnd in range(ROUNDS):
            x_round = keep.tile([P, ROUND_TILES, DIM], BF16, name="x_round%d" % rnd)
            x_rows.append(x_round)

        def load_x(rnd):
            b, s0 = rnd // ROUNDS_PER_BATCH, (rnd % ROUNDS_PER_BATCH) * ROUND_TILES
            nc.sync.dma_start(out=x_rows[rnd][:], in_=x_view[b, :, s0 : s0 + ROUND_TILES, :])

        load_x(0)

        wa_rows = keep.tile([P, PACK, DIM], BF16)
        wa_view = wq_a.rearrange("(r t) k -> r t k", t=PACK)
        for t in range(0, PACK, 2):
            nc.sync.dma_start(out=wa_rows[:, t : t + 2, :], in_=wa_view[:, t : t + 2, :])

        load_x(1)

        wb_rows = keep.tile([P, HEADS + 1, Q_LORA], BF16)
        wb_heads = wq_b.rearrange("(h d) k -> d h k", h=HEADS)
        nc.sync.dma_start(out=wb_rows[:, 0:HEADS, :], in_=wb_heads[0:NOPE, :, :])
        for h in range(HEADS):
            nc.sync.dma_start(
                out=wb_rows[h * ROPE : (h + 1) * ROPE, HEADS, :],
                in_=wb_heads[NOPE : NOPE + ROPE, h, :],
            )
        for rnd in range(2, ROUNDS):
            load_x(rnd)

        gain_row = keep.tile([P, Q_LORA], BF16)
        nc.gpsimd.memset(gain_row[:], 0.0)
        nc.scalar.dma_start(out=gain_row[0:1, :], in_=q_norm_w.rearrange("(o n) -> o n", o=1))
        cos_rows = keep.tile([P, SEQ_TILES, ROPE // 2], BF16)
        sin_rows = keep.tile([P, SEQ_TILES, ROPE // 2], BF16)
        nc.scalar.dma_start(
            out=cos_rows[:], in_=freqs_cos.rearrange("(p s) f -> p s f", s=SEQ_TILES)
        )
        nc.scalar.dma_start(
            out=sin_rows[:], in_=freqs_sin.rearrange("(p s) f -> p s f", s=SEQ_TILES)
        )

        ident_f32 = keep.tile([P, P], F32)
        make_identity(nc, ident_f32[:])
        ident_bf16 = keep.tile([P, P], BF16)
        make_identity(nc, ident_bf16[:])
        ones = keep.tile([P, P], BF16)
        nc.gpsimd.memset(ones[:], 1.0)

        warm = keep.tile([P, 1], F32)
        nc.scalar.activation(out=warm[:], in_=ones[:, 0:1], func=ACT.Abs_reciprocal_sqrt)

        rot = keep.tile([P, SEQ_TILES, 2, ROPE], F32)

        def prepare_rotation():
            rot_pairs = rot[:].rearrange("p s c (f e) -> p s c f e", e=2)
            nc.vector.tensor_copy(
                out=rot_pairs[:, :, 0, :, :],
                in_=cos_rows[:].unsqueeze(3).to_broadcast([P, SEQ_TILES, ROPE // 2, 2]),
            )
            nc.vector.tensor_scalar_mul(
                out=rot_pairs[:, :, 1, :, 0], in0=sin_rows[:], scalar1=-1.0
            )
            nc.vector.tensor_copy(out=rot_pairs[:, :, 1, :, 1], in_=sin_rows[:])

        def idle_bank(which, blocks):
            pool, tag = (
                (ps_qnt, "qnt"),
                (ps_nope, "nope_bank"),
                (ps_rope, "rope_bank"),
                (ps_ql, "ql"),
            )[which]
            return pool.tile([P, blocks, P], F32, tag=tag, name="weight_bank")

        def turn_words(bank, word_blocks):
            for slot, block in enumerate(word_blocks):
                nc.tensor.transpose(bank[:, slot, :], block, ident_f32[:])

        def blocks_of_row_words(words):
            return [words[:, slot * P : (slot + 1) * P] for slot in range(WORD_BLOCKS)]

        wa_codes = keep.tile([P, PASSES_1, Q_LORA], U32, align_bytes=64)
        wa_scales = keep.tile([P, PASSES_1, Q_LORA], U8, align_bytes=64)
        gain = keep.tile([P, Q_LORA], F32)

        def prepare_wq_a():
            grouped = keep.tile([P, PASSES_1 * Q_LORA * PACK], BF16, align_bytes=64, name="wa_grouped")
            grouped_words = grouped[:].bitcast(F32).rearrange(
                "p (g n u) -> p g n u", g=PASSES_1, u=2
            )
            for t in range(PACK):
                bank = idle_bank(t, WORD_BLOCKS)
                turn_words(bank, blocks_of_row_words(wa_rows[:, t, :].bitcast(F32)))
                copy_out(
                    t,
                    out=grouped_words[:, :, t * P : (t + 1) * P, :],
                    in_=bank[:].rearrange("p (g u) r -> p g r u", u=2),
                )
                if t % 2 == 1:
                    cols = slice((t - 1) * P, (t + 1) * P)
                    for g in range(PASSES_1):
                        first = (g * Q_LORA + (t - 1) * P) * PACK
                        nc.vector.quantize_mx(
                            out=wa_codes[:, g, cols].bitcast(FP8X4),
                            scales=wa_scales[:, g, cols],
                            in_=grouped[:, first : first + 2 * P * PACK],
                        )
            spread = ps_ql.tile([P, Q_LORA], F32, tag="ql")
            nc.tensor.matmul(out=spread[:], lhsT=ones[:], rhs=gain_row[:], start=True, stop=True)
            nc.scalar.copy(
                out=gain[:].rearrange("p (t r) -> p t r", t=PACK),
                in_=spread[:].rearrange("p (r t) -> p t r", t=PACK),
            )

        wb_codes = keep.tile([P, Q_COLS], U32, align_bytes=64)
        wb_scales = keep.tile([P, Q_COLS], U8, align_bytes=64)

        def prepare_wq_b():
            grouped = keep.tile([P, Q_COLS * PACK], BF16, align_bytes=64, name="wb_grouped")
            grouped_words = grouped[:].bitcast(F32).rearrange("p (n u) -> p n u", u=2)

            def every_second_word(i):
                words = wb_rows[:, i, :].bitcast(F32).rearrange("r (p u) -> r u p", u=2)
                return [words[:, u, :] for u in range(2)]

            bank = idle_bank(1, 2 * HEADS)
            turn_words(bank, every_second_word(0) + every_second_word(1))
            nc.scalar.copy(
                out=grouped_words[:, 0:NOPE_COLS, :].rearrange("p (i r) u -> p i r u", i=HEADS),
                in_=bank[:].rearrange("p (i u) r -> p i r u", u=2),
            )
            bank = idle_bank(2, 2)
            turn_words(bank, every_second_word(HEADS))
            nc.scalar.copy(
                out=grouped_words[:, NOPE_COLS : NOPE_COLS + ROPE_COLS, :],
                in_=bank[:].rearrange("p u r -> p r u"),
            )
            swapped = grouped_words[:, NOPE_COLS + ROPE_COLS : Q_COLS, :].rearrange(
                "p (m e) u -> p m e u", e=2
            )
            row_pairs = bank[:].rearrange("p u (m e) -> p m e u", e=2)
            for e in range(2):
                nc.scalar.copy(out=swapped[:, :, 1 - e, :], in_=row_pairs[:, :, e, :])
            nc.vector.quantize_mx(
                out=wb_codes[:].bitcast(FP8X4), scales=wb_scales[:], in_=grouped[:]
            )

        x_grouped, x_mx, ql_banks, rstd_of = {}, {}, {}, {}
        qn_of, qn_grouped, qn_mx, q_banks = {}, {}, {}, {}

        def turn_x(rnd):
            grouped = pair.tile([P, ROUND_TILES * DIM], BF16, align_bytes=64, tag="x_grouped")
            grouped_words = grouped[:].bitcast(F32).rearrange(
                "p (j g r u) -> p j g r u", j=ROUND_TILES, g=PASSES_1, u=2
            )
            for j in range(ROUND_TILES):
                bank = ps_words.tile([P, WORD_BLOCKS, P], F32, tag="words")
                turn_words(bank, blocks_of_row_words(x_rows[rnd][:, j, :].bitcast(F32)))
                copy_out(
                    j, out=grouped_words[:, j], in_=bank[:].rearrange("p (g u) r -> p g r u", u=2)
                )
            x_grouped[rnd] = grouped

        def quantise_x(rnd):
            codes = ring.tile([P, ROUND_TILES * PASSES_1 * P], U32, align_bytes=64, tag="x_codes")
            scales = ring.tile([P, ROUND_TILES * PASSES_1 * P], U8, align_bytes=64, tag="x_scales")
            nc.vector.quantize_mx(
                out=codes[:].bitcast(FP8X4), scales=scales[:], in_=x_grouped[rnd][:]
            )
            x_mx[rnd] = (codes, scales)

        def product_1(rnd):
            codes, scales = x_mx[rnd]
            sum_sq = ring.tile([P, ROUND_TILES], F32, tag="sum_sq")
            ql_banks[rnd] = []
            for j in range(ROUND_TILES):
                ql = ps_ql.tile([P, Q_LORA], F32, tag="ql")
                for g in range(PASSES_1):
                    tok = slice((j * PASSES_1 + g) * P, (j * PASSES_1 + g + 1) * P)
                    nc.tensor.matmul_mx(
                        out=ql[:],
                        lhsT=codes[:, tok].bitcast(FP8X4),
                        lhsT_scale=scales[:, tok],
                        rhs=wa_codes[:, g, :].bitcast(FP8X4),
                        rhs_scale=wa_scales[:, g, :],
                        start=(g == 0),
                        stop=(g == PASSES_1 - 1),
                    )
                squares = pair.tile([P, Q_LORA], BF16, tag="squares")
                nc.scalar.activation(
                    out=squares[:], in_=ql[:], func=ACT.Square, accum_out=sum_sq[:, j : j + 1]
                )
                ql_banks[rnd].append(ql)
            rstd = ring.tile([P, ROUND_TILES], F32, tag="rstd")
            nc.scalar.activation(
                out=rstd[:],
                in_=sum_sq[:],
                func=ACT.Abs_reciprocal_sqrt,
                bias=EPS,
                scale=1.0 / Q_LORA,
            )
            rstd_of[rnd] = rstd

        def normalise(rnd):
            rstd = rstd_of[rnd]
            qn = ring.tile([P, ROUND_TILES, Q_LORA], BF16, tag="qn")
            for j in range(ROUND_TILES):
                nc.vector.scalar_tensor_tensor(
                    out=qn[:, j, :],
                    in0=ql_banks[rnd][j][:],
                    scalar=rstd[:, j : j + 1],
                    in1=gain[:],
                    op0=ALU.mult,
                    op1=ALU.mult,
                )
            qn_of[rnd] = qn

        def turn_qn(rnd):
            qnt = ps_qnt.tile([P, ROUND_TILES, PACK, P], BF16, tag="qnt")
            for j in range(ROUND_TILES):
                for t in range(PACK):
                    nc.tensor.transpose(
                        qnt[:, j, t, :], qn_of[rnd][:, j, t * P : (t + 1) * P], ident_bf16[:]
                    )
            grouped = pair.tile([P, ROUND_TILES * Q_LORA], BF16, align_bytes=64, tag="qn_grouped")
            nc.scalar.copy(
                out=grouped[:].rearrange("p (j r t) -> p j r t", j=ROUND_TILES, t=PACK),
                in_=qnt[:].rearrange("p j t r -> p j r t"),
            )
            qn_grouped[rnd] = grouped

        def quantise_qn(rnd):
            codes = ring.tile([P, ROUND_TILES * P], U32, align_bytes=64, tag="qn_codes")
            scales = ring.tile([P, ROUND_TILES * P], U8, align_bytes=64, tag="qn_scales")
            nc.vector.quantize_mx(
                out=codes[:].bitcast(FP8X4), scales=scales[:], in_=qn_grouped[rnd][:]
            )
            qn_mx[rnd] = (codes, scales)

        def product_2(rnd):
            codes, scales = qn_mx[rnd]
            nope_bank = ps_nope.tile([P, ROUND_TILES, NOPE_COLS], F32, tag="nope_bank")
            rope_bank = ps_rope.tile([P, ROUND_TILES, 2 * ROPE_COLS], F32, tag="rope_bank")
            for j in range(ROUND_TILES):
                tok = slice(j * P, (j + 1) * P)
                for bank, cols in (
                    (nope_bank, slice(0, NOPE_COLS)),
                    (rope_bank, slice(NOPE_COLS, Q_COLS)),
                ):
                    nc.tensor.matmul_mx(
                        out=bank[:, j, :],
                        lhsT=codes[:, tok].bitcast(FP8X4),
                        lhsT_scale=scales[:, tok],
                        rhs=wb_codes[:, cols].bitcast(FP8X4),
                        rhs_scale=wb_scales[:, cols],
                        start=True,
                        stop=True,
                    )
            q_banks[rnd] = (nope_bank, rope_bank)

        def finish(rnd):
            b, s0 = rnd // ROUNDS_PER_BATCH, (rnd % ROUNDS_PER_BATCH) * ROUND_TILES
            nope_bank, rope_bank = q_banks[rnd]
            nope = ring.tile([P, ROUND_TILES, NOPE_COLS], F32, tag="nope")
            nc.scalar.copy(out=nope[:], in_=nope_bank[:])
            terms = ring.tile([P, ROUND_TILES, 2 * ROPE_COLS], F32, tag="terms")
            nc.vector.tensor_tensor(
                out=terms[:].rearrange("p j (c h d) -> p (j c) h d", c=2, h=HEADS),
                in0=rope_bank[:].rearrange("p j (c h d) -> p (j c) h d", c=2, h=HEADS),
                in1=rot[:, s0 : s0 + ROUND_TILES]
                .rearrange("p s c d -> p (s c) d")
                .unsqueeze(2)
                .to_broadcast([P, 2 * ROUND_TILES, HEADS, ROPE]),
                op=ALU.mult,
            )
            rope = ring.tile([P, ROUND_TILES, ROPE_COLS], F32, tag="rope")
            nc.gpsimd.tensor_tensor(
                out=rope[:],
                in0=terms[:, :, 0:ROPE_COLS],
                in1=terms[:, :, ROPE_COLS : 2 * ROPE_COLS],
                op=ALU.add,
            )
            nc.sync.dma_start(out=nope_view[b, :, s0 : s0 + ROUND_TILES, :], in_=nope[:])
            nc.sync.dma_start(out=rope_view[b, :, s0 : s0 + ROUND_TILES, :], in_=rope[:])

        def run(stage_of_round, rnd):
            if 0 <= rnd < ROUNDS:
                stage_of_round(rnd)

        for step in range(ROUNDS + FINISH_LAG):
            run(finish, step - FINISH_LAG)
            run(normalise, step - NORMALISE_LAG)
            run(turn_x, step)
            run(turn_qn, step - TURN_QN_LAG)
            run(quantise_qn, step - TURN_QN_LAG)
            run(quantise_x, step)
            if step == PREPARE_WQ_A_STEP:
                prepare_wq_a()
            if step == PREPARE_ROTATION_STEP:
                prepare_rotation()
            if step == PREPARE_WQ_B_STEP:
                prepare_wq_b()
            run(product_1, step - PRODUCT_1_LAG)
            run(product_2, step - PRODUCT_2_LAG)
